import numpy as np
import ml_dtypes


def mxq(x, axis, fmt="e4m3"):
    dtype, down = {"e4m3": (ml_dtypes.float8_e4m3fn, 7), "e5m2": (ml_dtypes.float8_e5m2, 14)}[fmt]
    v = np.moveaxis(np.asarray(x, np.float32).astype(ml_dtypes.bfloat16).astype(np.float64), axis, -1)
    blocks = v.reshape(v.shape[:-1] + (-1, 32))
    amax = np.abs(blocks).max(-1, keepdims=True)
    byte = np.maximum(np.where(amax > 0, np.frexp(amax)[1] - 1 + 127, 0) - down, 1)
    scale = np.exp2(byte - 127.0)
    codes = (blocks / scale).astype(np.float32).astype(dtype).astype(np.float64)
    return np.moveaxis((codes * scale).reshape(v.shape), -1, axis)


WIDE = False


def mx_kscale(k):
    if not WIDE:
        return np.ones(k)
    levels = np.array([10, -10, 5, -5, 0])
    a = np.random.permutation(np.resize(levels, k // 512 * 4)).reshape(k // 512, 4)
    idx = np.arange(k)
    return np.exp2(a[idx // 512, idx % 128 // 32])


BF16 = ml_dtypes.bfloat16


def bf(x):
    return np.asarray(x, np.float32).astype(BF16)


def f64(x):
    return np.asarray(x).astype(np.float64)


E2M1 = np.array([0.0, 0.5, 1.0, 1.5, 2.0, 3.0, 4.0, 6.0, -0.0, -0.5, -1.0, -1.5, -2.0, -3.0, -4.0, -6.0])


def pack_weight(w, fmt):
    k, n = w.shape
    w = f64(bf(w)).reshape(k // 32, 32, n)
    amax = np.abs(w).max(1)
    if fmt == "e4m3":
        byte = np.frexp(amax)[1] - 1 + 127 - 7
    else:
        mant, ex = np.frexp(amax / 6.0)
        byte = np.where(mant > 0.5, ex, ex - 1) + 127
    byte = np.clip(np.where(amax > 0, byte, 1), 1, 254)
    scaled = (w * np.exp2(127.0 - byte)[:, None, :]).reshape(k, n).astype(np.float32)
    by_word = np.ascontiguousarray(scaled.reshape(k // 512, 128, 4, n).transpose(0, 1, 3, 2))
    if fmt == "e4m3":
        words = by_word.astype(ml_dtypes.float8_e4m3fn).view(np.uint8)
    else:
        c = by_word.astype(ml_dtypes.float4_e2m1fn).view(np.uint8) & 0xF
        words = c[..., 0::2] | (c[..., 1::2] << 4)
    return np.ascontiguousarray(words), np.ascontiguousarray(byte.astype(np.uint8).reshape(k // 512, 16, n))


def unpack_weight(words, scales, fmt):
    g, p, n, _ = words.shape
    if fmt == "e4m3":
        vals = np.ascontiguousarray(words).view(ml_dtypes.float8_e4m3fn).astype(np.float64)
    else:
        nib = np.empty((g, p, n, 4), np.uint8)
        nib[..., 0::2] = words & 0xF
        nib[..., 1::2] = words >> 4
        vals = E2M1[nib]
    vals = vals * np.repeat(np.exp2(scales.astype(np.float64) - 127.0), 8, axis=1)[..., None]
    return vals.transpose(0, 1, 3, 2).reshape(g * 512, n)


B, S, H, D, M = 2, 2048, 2, 512, 512
E = H * D
R = B * S
EPS = 1e-6
QK = np.sqrt(1.5) / D ** 0.25


def setup_inputs():
    s = mx_kscale(M)
    q = np.random.standard_normal((B, S, H, D)) * QK
    k = np.random.standard_normal((H, M, D)) * QK
    q[..., 0] = np.log(2.0)
    k[:, :, 0] += np.log2(s)[None, :]
    v = np.random.standard_normal((H, M, D)) / s[None, :, None] * np.mean(s)
    v_words, v_scales = pack_weight(v.reshape(-1, D), "e4m3")
    return {"q_scaled": bf(q),
            "k": bf(k),
            "v_words": v_words,
            "v_scales": v_scales,
            "norm_retrieved_w": bf(1.0 + 0.1 * np.random.standard_normal(E)),
            "query_input": bf(np.random.standard_normal((B, S, E)))}


def reference(q_scaled, k, v_words, v_scales, norm_retrieved_w, query_input):
    q = f64(q_scaled).reshape(R, H, D)
    kk = f64(k)
    vv = unpack_weight(v_words, v_scales, "e4m3").reshape(H, M, D)
    heads = []
    for h in range(H):
        s = q[:, h, :] @ kk[h].T
        e = np.exp(s - s.max(1, keepdims=True))
        heads.append((mxq(e, 1, "e4m3") @ vv[h]) / e.sum(1, keepdims=True))
    attn_flat = np.concatenate(heads, 1)
    retrieved = attn_flat * (1.0 / np.sqrt(np.mean(attn_flat * attn_flat, 1, keepdims=True) + EPS)) * f64(norm_retrieved_w)
    return (retrieved + f64(query_input).reshape(R, E)).reshape(B, S, E)

@@ -1,0 +1,277 @@
+from contextlib import ExitStack
+
+import concourse.masks as masks
+import concourse.mybir as mybir
+
+F32 = mybir.dt.float32
+BF16 = mybir.dt.bfloat16
+I32 = mybir.dt.int32
+U32 = mybir.dt.uint32
+U8 = mybir.dt.uint8
+FP8X4 = mybir.dt.float8_e4m3fn_x4
+ALU = mybir.AluOpType
+ACT = mybir.ActivationFunctionType
+AXIS = mybir.AxisListType
+
+P = 128
+HEADS = 2
+D = 512
+SLOTS = 512
+E = HEADS * D
+ROWS = 2 * 2048
+EPS = 1e-6
+D_CHUNKS = D // P
+PACK = 4
+PAIRS = PACK // 2
+BLOCK_TILES = 4
+N_BLOCKS = ROWS // (P * BLOCK_TILES)
+N_TILES = ROWS // P
+
+FLOPS = 2 * 2 * ROWS * HEADS * D * SLOTS
+
+
+def tile_hopfieldmemorylayer_pb_t_e_kernel(
+    tc, q_scaled, k, v_words, v_scales, norm_retrieved_w, query_input, out
+):
+    nc = tc.nc
+
+    by_block = "(n p t) f -> n p t f"
+    q_blocks = q_scaled.rearrange("b s h d -> (b s) (h d)").rearrange(by_block, p=P, t=BLOCK_TILES)
+    x_blocks = query_input.rearrange("b s f -> (b s) f").rearrange(by_block, p=P, t=BLOCK_TILES)
+    out_blocks = out.rearrange("b s f -> (b s) f").rearrange(by_block, p=P, t=BLOCK_TILES)
+
+    with ExitStack() as ctx:
+        keep = ctx.enter_context(tc.tile_pool(name="keep", bufs=1))
+        work = ctx.enter_context(tc.tile_pool(name="work", bufs=4))
+        stats = ctx.enter_context(tc.tile_pool(name="stats", bufs=8))
+        psum_turn = ctx.enter_context(tc.psum_pool(name="psum_turn", bufs=1))
+        psum_scores = ctx.enter_context(tc.psum_pool(name="psum_scores", bufs=3))
+        psum_acc = ctx.enter_context(tc.psum_pool(name="psum_acc", bufs=3))
+
+        v_planes = keep.tile([P, HEADS, D], U8, align_bytes=64)
+        nc.vector.memset(v_planes[:].bitcast(I32), 0)
+        minus_half = keep.tile([P, 1], F32)
+        nc.vector.memset(minus_half[:], -0.5)
+        ident_bf = keep.tile([P, P], BF16)
+        masks.make_identity(nc, ident_bf[:])
+        ident_f32 = keep.tile([P, P], F32)
+        masks.make_identity(nc, ident_f32[:])
+
+        k_sb = keep.tile([P, HEADS, PACK, D], BF16)
+        nc.sync.dma_start(out=k_sb[:], in_=k.rearrange("h (p a) d -> p h a d", a=PACK))
+        q_sb = []
+        x_sb = []
+        for n in range(N_BLOCKS):
+            q_sb.append(keep.tile([P, BLOCK_TILES, E], BF16, name="q_sb%d" % n))
+            x_sb.append(keep.tile([P, BLOCK_TILES, E], BF16, name="x_sb%d" % n))
+        nc.sync.dma_start(out=q_sb[0][:], in_=q_blocks[0])
+        v_codes = keep.tile([P, HEADS, D], U32, align_bytes=64)
+        nc.sync.dma_start(
+            out=v_codes[:].bitcast(I32),
+            in_=v_words.rearrange("g p n t -> p g (n t)").bitcast(I32),
+        )
+        for quadrant in range(4):
+            nc.sync.dma_start(
+                out=v_planes[32 * quadrant : 32 * quadrant + 4].bitcast(I32),
+                in_=v_scales[:, 4 * quadrant : 4 * quadrant + 4, :]
+                .rearrange("g r n -> r g n")
+                .bitcast(I32),
+            )
+        gain_bf = keep.tile([P, E], BF16)
+        nc.sync.dma_start(out=gain_bf[:], in_=norm_retrieved_w.partition_broadcast(P))
+        for n in range(N_BLOCKS):
+            if n + 1 < N_BLOCKS:
+                nc.sync.dma_start(out=q_sb[n + 1][:], in_=q_blocks[n + 1])
+            nc.sync.dma_start(out=x_sb[n][:], in_=x_blocks[n])
+
+        table_warmer = keep.tile([P, 1], F32)
+        nc.scalar.activation(out=table_warmer[:], in_=minus_half[:], func=ACT.Exp)
+        gain32 = keep.tile([P, HEADS, D], F32)
+        nc.scalar.mul(gain32[:].rearrange("p h d -> p (h d)"), gain_bf[:], float(E) ** 0.5)
+
+        kT = keep.tile([P, HEADS, D_CHUNKS, SLOTS], BF16)
+        for h in range(HEADS):
+            for half in range(2):
+                kT_ps = psum_scores.tile([P, 2, PACK, P], BF16, tag="s_ps")
+                for j in range(2):
+                    c = 2 * half + j
+                    for a in range(PACK):
+                        nc.tensor.transpose(
+                            kT_ps[:, j, a, :], k_sb[:, h, a, c * P : (c + 1) * P], ident_bf[:]
+                        )
+                for j in range(2):
+                    c = 2 * half + j
+                    copy = nc.vector.tensor_copy if j == 0 else nc.scalar.copy
+                    copy(
+                        out=kT[:, h, c, :].rearrange("d (u p i) -> d u p i", u=PAIRS, i=2),
+                        in_=kT_ps[:, j].rearrange("d (u i) p -> d u p i", i=2),
+                    )
+
+        qT_ps, qT, s_ps, neg_max, row_sum, e_sb, eT_ps = {}, {}, {}, {}, {}, {}, {}
+        grouped, e_codes, e_scales, inv_sum, acc, sum_sq, scaled, inv_rms = {}, {}, {}, {}, {}, {}, {}, {}
+
+        def live(i):
+            return 0 <= i < N_TILES
+
+        def turn_q(i, j):
+            if j == 0:
+                qT_ps[i] = psum_turn.tile([P, HEADS * D_CHUNKS, P], BF16, name="qT_ps")
+            rows = q_sb[i // BLOCK_TILES][:, i % BLOCK_TILES, :]
+            nc.tensor.transpose(qT_ps[i][:, j, :], rows[:, j * P : (j + 1) * P], ident_bf[:])
+
+        def keep_qT(i):
+            qT[i] = work.tile([P, HEADS * D_CHUNKS, P], BF16, name="qT")
+            nc.scalar.copy(out=qT[i][:], in_=qT_ps[i][:])
+
+        def score(i, h, c):
+            if c == 0:
+                s_ps[i, h] = psum_scores.tile([P, SLOTS], F32, name="s_ps")
+            nc.tensor.matmul(
+                s_ps[i, h][:],
+                lhsT=qT[i][:, D_CHUNKS * h + c, :],
+                rhs=kT[:, h, c, :],
+                start=(c == 0),
+                stop=(c == D_CHUNKS - 1),
+            )
+
+        def softmax_numerator(i, h):
+            if h == 0:
+                neg_max[i] = stats.tile([P, HEADS], F32, name="neg_max")
+                row_sum[i] = stats.tile([P, HEADS], F32, name="row_sum")
+                e_sb[i] = work.tile([P, HEADS, SLOTS], BF16, name="e_sb")
+            nc.vector.tensor_reduce(
+                out=neg_max[i][:, h : h + 1], in_=s_ps[i, h][:], axis=AXIS.X, op=ALU.max, negate=True
+            )
+            nc.scalar.activation(
+                out=e_sb[i][:, h, :],
+                in_=s_ps[i, h][:],
+                func=ACT.Exp,
+                bias=neg_max[i][:, h : h + 1],
+                scale=1.0,
+                accum_out=row_sum[i][:, h : h + 1],
+            )
+
+        def turn_e(i, h, u):
+            if h == 0 and u == 0:
+                eT_ps[i] = psum_turn.tile([P, HEADS, PAIRS, P], F32, name="eT_ps")
+            words = e_sb[i][:, h, :].bitcast(F32)
+            nc.tensor.transpose(eT_ps[i][:, h, u, :], words[:, u * P : (u + 1) * P], ident_f32[:])
+
+        def group_e(i):
+            grouped[i] = work.tile([P, HEADS, P, PACK], BF16, name="grouped", align_bytes=64)
+            nc.scalar.copy(
+                out=grouped[i][:]
+                .rearrange("p h r t -> p (h r t)")
+                .bitcast(F32)
+                .rearrange("p (h r u) -> p h r u", h=HEADS, u=PAIRS),
+                in_=eT_ps[i][:].rearrange("p h u r -> p h r u"),
+            )
+
+        def quantise_e(i):
+            e_codes[i] = work.tile([P, HEADS * P], U32, name="e_codes", align_bytes=64)
+            e_scales[i] = work.tile([P, HEADS * P], U8, name="e_scales", align_bytes=64)
+            nc.vector.quantize_mx(
+                out=e_codes[i][:].bitcast(FP8X4),
+                scales=e_scales[i][:],
+                in_=grouped[i][:].rearrange("p h r t -> p (h r t)"),
+            )
+
+        def invert_row_sum(i):
+            inv_sum[i] = stats.tile([P, HEADS], F32, name="inv_sum")
+            nc.vector.reciprocal(out=inv_sum[i][:], in_=row_sum[i][:])
+
+        def retrieve(i, h):
+            acc[i, h] = psum_acc.tile([P, D], F32, name="acc")
+            rows = slice(h * P, (h + 1) * P)
+            nc.tensor.matmul_mx(
+                out=acc[i, h][:],
+                lhsT=e_codes[i][:, rows].bitcast(FP8X4),
+                lhsT_scale=e_scales[i][:, rows],
+                rhs=v_codes[:, h, :].bitcast(FP8X4),
+                rhs_scale=v_planes[:, h, :],
+                start=True,
+                stop=True,
+            )
+
+        def apply_gain(i, h):
+            nc.vector.scalar_tensor_tensor(
+                out=scaled[i][:, h, :],
+                in0=acc[i, h][:],
+                scalar=inv_sum[i][:, h : h + 1],
+                in1=gain32[:, h, :],
+                op0=ALU.mult,
+                op1=ALU.mult,
+            )
+
+        def sum_squares(i, h):
+            squares = work.tile([P, D], BF16, name="squares")
+            nc.scalar.activation(
+                out=squares[:],
+                in_=acc[i, h][:],
+                func=ACT.Square,
+                scale=inv_sum[i][:, h : h + 1],
+                accum_out=sum_sq[i][:, h : h + 1],
+            )
+
+        def leave_psum(i):
+            scaled[i] = work.tile([P, HEADS, D], F32, name="scaled")
+            sum_sq[i] = stats.tile([P, HEADS], F32, name="sum_sq")
+            apply_gain(i, 0)
+            sum_squares(i, 1)
+            sum_squares(i, 0)
+            apply_gain(i, 1)
+            total = stats.tile([P, 1], F32, name="total")
+            nc.gpsimd.tensor_scalar(
+                out=total[:],
+                in0=sum_sq[i][:, 0:1],
+                scalar1=sum_sq[i][:, 1:2],
+                scalar2=E * EPS,
+                op0=ALU.add,
+                op1=ALU.add,
+            )
+            inv_rms[i] = stats.tile([P, 1], F32, name="inv_rms")
+            nc.gpsimd.tensor_tensor(out=inv_rms[i][:], in0=total[:], in1=minus_half[:], op=ALU.pow)
+
+        def finish(i):
+            row = scaled[i][:].rearrange("p h d -> p (h d)")
+            nc.vector.scalar_tensor_tensor(
+                out=row,
+                in0=row,
+                scalar=inv_rms[i][:, 0:1],
+                in1=x_sb[i // BLOCK_TILES][:, i % BLOCK_TILES, :],
+                op0=ALU.mult,
+                op1=ALU.add,
+            )
+            nc.sync.dma_start(out=out_blocks[i // BLOCK_TILES][:, i % BLOCK_TILES, :], in_=row)
+
+        for i in range(-1, N_TILES + 5):
+            if live(i - 4):
+                leave_psum(i - 4)
+            for c in range(D_CHUNKS):
+                if live(i):
+                    score(i, 0, c)
+                if live(i + 1):
+                    turn_q(i + 1, 2 * c)
+                    turn_q(i + 1, 2 * c + 1)
+            for c in range(D_CHUNKS):
+                if live(i):
+                    score(i, 1, c)
+                if live(i - 2) and c < HEADS:
+                    turn_e(i - 2, c, 0)
+                    turn_e(i - 2, c, 1)
+            for h in range(HEADS):
+                if live(i - 3):
+                    retrieve(i - 3, h)
+            if live(i + 1):
+                keep_qT(i + 1)
+            if live(i):
+                softmax_numerator(i, 0)
+            if live(i - 5):
+                finish(i - 5)
+            if live(i - 2):
+                group_e(i - 2)
+            if live(i):
+                softmax_numerator(i, 1)
+            if live(i - 2):
+                invert_row_sum(i - 2)
+                quantise_e(i - 2)

@@ -47,6 +47,7 @@ def tile_hopfieldmemorylayer_pb_t_e_kernel(
         psum_turn = ctx.enter_context(tc.psum_pool(name="psum_turn", bufs=1))
         psum_scores = ctx.enter_context(tc.psum_pool(name="psum_scores", bufs=3))
         psum_acc = ctx.enter_context(tc.psum_pool(name="psum_acc", bufs=3))
+        ctx.enter_context(tc.manual_schedule())
 
         v_planes = keep.tile([P, HEADS, D], U8, align_bytes=64)
         nc.vector.memset(v_planes[:].bitcast(I32), 0)
@@ -79,15 +80,20 @@ def tile_hopfieldmemorylayer_pb_t_e_kernel(
             )
         gain_bf = keep.tile([P, E], BF16)
         nc.sync.dma_start(out=gain_bf[:], in_=norm_retrieved_w.partition_broadcast(P))
-        for n in range(N_BLOCKS):
-            if n + 1 < N_BLOCKS:
-                nc.sync.dma_start(out=q_sb[n + 1][:], in_=q_blocks[n + 1])
-            nc.sync.dma_start(out=x_sb[n][:], in_=x_blocks[n])
+        nc.sync.dma_start(out=q_sb[1][:], in_=q_blocks[1])
+        nc.sync.dma_start(out=x_sb[0][:], in_=x_blocks[0])
 
         table_warmer = keep.tile([P, 1], F32)
         nc.scalar.activation(out=table_warmer[:], in_=minus_half[:], func=ACT.Exp)
         gain32 = keep.tile([P, HEADS, D], F32)
-        nc.scalar.mul(gain32[:].rearrange("p h d -> p (h d)"), gain_bf[:], float(E) ** 0.5)
+        nc.gpsimd.tensor_scalar(
+            out=gain32[:].rearrange("p h d -> p (h d)"),
+            in0=gain_bf[:],
+            scalar1=float(E) ** 0.5,
+            scalar2=0.0,
+            op0=ALU.mult,
+            op1=ALU.add,
+        )
 
         kT = keep.tile([P, HEADS, D_CHUNKS, SLOTS], BF16)
         for h in range(HEADS):
@@ -245,6 +251,12 @@ def tile_hopfieldmemorylayer_pb_t_e_kernel(
             nc.sync.dma_start(out=out_blocks[i // BLOCK_TILES][:, i % BLOCK_TILES, :], in_=row)
 
         for i in range(-1, N_TILES + 5):
+            if live(i) and i % BLOCK_TILES == 0:
+                n = i // BLOCK_TILES
+                if n + 2 < N_BLOCKS:
+                    nc.sync.dma_start(out=q_sb[n + 2][:], in_=q_blocks[n + 2])
+                if n + 1 < N_BLOCKS:
+                    nc.sync.dma_start(out=x_sb[n + 1][:], in_=x_blocks[n + 1])
             if live(i - 4):
                 leave_psum(i - 4)
             for c in range(D_CHUNKS):

@@ -26,6 +26,7 @@ PAIRS = PACK // 2
 BLOCK_TILES = 4
 N_BLOCKS = ROWS // (P * BLOCK_TILES)
 N_TILES = ROWS // P
+GAPS = D_CHUNKS - 1
 
 FLOPS = 2 * 2 * ROWS * HEADS * D * SLOTS
 
@@ -43,6 +44,7 @@ def tile_hopfieldmemorylayer_pb_t_e_kernel(
     with ExitStack() as ctx:
         keep = ctx.enter_context(tc.tile_pool(name="keep", bufs=1))
         work = ctx.enter_context(tc.tile_pool(name="work", bufs=4))
+        results = ctx.enter_context(tc.tile_pool(name="results", bufs=6))
         stats = ctx.enter_context(tc.tile_pool(name="stats", bufs=8))
         psum_turn = ctx.enter_context(tc.psum_pool(name="psum_turn", bufs=1))
         psum_scores = ctx.enter_context(tc.psum_pool(name="psum_scores", bufs=3))
@@ -57,15 +59,20 @@ def tile_hopfieldmemorylayer_pb_t_e_kernel(
         masks.make_identity(nc, ident_bf[:])
         ident_f32 = keep.tile([P, P], F32)
         masks.make_identity(nc, ident_f32[:])
+        table_warmer = keep.tile([P, 1], F32)
+        nc.scalar.activation(out=table_warmer[:], in_=minus_half[:], func=ACT.Exp)
 
-        k_sb = keep.tile([P, HEADS, PACK, D], BF16)
-        nc.sync.dma_start(out=k_sb[:], in_=k.rearrange("h (p a) d -> p h a d", a=PACK))
         q_sb = []
         x_sb = []
         for n in range(N_BLOCKS):
             q_sb.append(keep.tile([P, BLOCK_TILES, E], BF16, name="q_sb%d" % n))
             x_sb.append(keep.tile([P, BLOCK_TILES, E], BF16, name="x_sb%d" % n))
-        nc.sync.dma_start(out=q_sb[0][:], in_=q_blocks[0])
+        k_sb = keep.tile([P, HEADS, PACK, D], BF16)
+        k_by_slot_group = k.rearrange("h (p a) d -> h p a d", a=PACK)
+        nc.sync.dma_start(out=k_sb[:, 0], in_=k_by_slot_group[0])
+        nc.sync.dma_start(out=q_sb[0][:, 0:1], in_=q_blocks[0][:, 0:1])
+        nc.sync.dma_start(out=k_sb[:, 1], in_=k_by_slot_group[1])
+        nc.sync.dma_start(out=q_sb[0][:, 1:], in_=q_blocks[0][:, 1:])
         v_codes = keep.tile([P, HEADS, D], U32, align_bytes=64)
         nc.sync.dma_start(
             out=v_codes[:].bitcast(I32),
@@ -82,9 +89,6 @@ def tile_hopfieldmemorylayer_pb_t_e_kernel(
         nc.sync.dma_start(out=gain_bf[:], in_=norm_retrieved_w.partition_broadcast(P))
         nc.sync.dma_start(out=q_sb[1][:], in_=q_blocks[1])
         nc.sync.dma_start(out=x_sb[0][:], in_=x_blocks[0])
-
-        table_warmer = keep.tile([P, 1], F32)
-        nc.scalar.activation(out=table_warmer[:], in_=minus_half[:], func=ACT.Exp)
         gain32 = keep.tile([P, HEADS, D], F32)
         nc.gpsimd.tensor_scalar(
             out=gain32[:].rearrange("p h d -> p (h d)"),
@@ -96,7 +100,8 @@ def tile_hopfieldmemorylayer_pb_t_e_kernel(
         )
 
         kT = keep.tile([P, HEADS, D_CHUNKS, SLOTS], BF16)
-        for h in range(HEADS):
+
+        def turn_keys(h):
             for half in range(2):
                 kT_ps = psum_scores.tile([P, 2, PACK, P], BF16, tag="s_ps")
                 for j in range(2):
@@ -105,19 +110,25 @@ def tile_hopfieldmemorylayer_pb_t_e_kernel(
                         nc.tensor.transpose(
                             kT_ps[:, j, a, :], k_sb[:, h, a, c * P : (c + 1) * P], ident_bf[:]
                         )
-                for j in range(2):
-                    c = 2 * half + j
-                    copy = nc.vector.tensor_copy if j == 0 else nc.scalar.copy
-                    copy(
-                        out=kT[:, h, c, :].rearrange("d (u p i) -> d u p i", u=PAIRS, i=2),
-                        in_=kT_ps[:, j].rearrange("d (u i) p -> d u p i", i=2),
-                    )
+                in_order = "d (u p i) -> d u p i"
+                as_turned = "d (u i) p -> d u p i"
+                nc.vector.tensor_copy(
+                    out=kT[:, h, 2 * half, :].rearrange(in_order, u=PAIRS, i=2),
+                    in_=kT_ps[:, 0].rearrange(as_turned, i=2),
+                )
+                nc.scalar.copy(
+                    out=kT[:, h, 2 * half + 1, :].rearrange(in_order, u=PAIRS, i=2),
+                    in_=kT_ps[:, 1].rearrange(as_turned, i=2),
+                )
 
         qT_ps, qT, s_ps, neg_max, row_sum, e_sb, eT_ps = {}, {}, {}, {}, {}, {}, {}
         grouped, e_codes, e_scales, inv_sum, acc, sum_sq, scaled, inv_rms = {}, {}, {}, {}, {}, {}, {}, {}
 
         def live(i):
             return 0 <= i < N_TILES
+
+        def at(j, lag):
+            return (j - lag) // HEADS, (j - lag) % HEADS
 
         def turn_q(i, j):
             if j == 0:
@@ -140,14 +151,17 @@ def tile_hopfieldmemorylayer_pb_t_e_kernel(
                 stop=(c == D_CHUNKS - 1),
             )
 
-        def softmax_numerator(i, h):
+        def row_max(i, h):
             if h == 0:
                 neg_max[i] = stats.tile([P, HEADS], F32, name="neg_max")
-                row_sum[i] = stats.tile([P, HEADS], F32, name="row_sum")
-                e_sb[i] = work.tile([P, HEADS, SLOTS], BF16, name="e_sb")
             nc.vector.tensor_reduce(
                 out=neg_max[i][:, h : h + 1], in_=s_ps[i, h][:], axis=AXIS.X, op=ALU.max, negate=True
             )
+
+        def exponentials(i, h):
+            if h == 0:
+                row_sum[i] = stats.tile([P, HEADS], F32, name="row_sum")
+                e_sb[i] = work.tile([P, HEADS, SLOTS], BF16, name="e_sb")
             nc.scalar.activation(
                 out=e_sb[i][:, h, :],
                 in_=s_ps[i, h][:],
@@ -200,6 +214,8 @@ def tile_hopfieldmemorylayer_pb_t_e_kernel(
             )
 
         def apply_gain(i, h):
+            if h == 0:
+                scaled[i] = results.tile([P, HEADS, D], F32, name="scaled")
             nc.vector.scalar_tensor_tensor(
                 out=scaled[i][:, h, :],
                 in0=acc[i, h][:],
@@ -210,6 +226,8 @@ def tile_hopfieldmemorylayer_pb_t_e_kernel(
             )
 
         def sum_squares(i, h):
+            if h == 0:
+                sum_sq[i] = stats.tile([P, HEADS], F32, name="sum_sq")
             squares = work.tile([P, D], BF16, name="squares")
             nc.scalar.activation(
                 out=squares[:],
@@ -218,72 +236,74 @@ def tile_hopfieldmemorylayer_pb_t_e_kernel(
                 scale=inv_sum[i][:, h : h + 1],
                 accum_out=sum_sq[i][:, h : h + 1],
             )
+            if h == HEADS - 1:
+                total = stats.tile([P, 1], F32, name="total")
+                nc.gpsimd.tensor_scalar(
+                    out=total[:],
+                    in0=sum_sq[i][:, 0:1],
+                    scalar1=sum_sq[i][:, 1:2],
+                    scalar2=E * EPS,
+                    op0=ALU.add,
+                    op1=ALU.add,
+                )
+                inv_rms[i] = stats.tile([P, 1], F32, name="inv_rms")
+                nc.gpsimd.tensor_tensor(out=inv_rms[i][:], in0=total[:], in1=minus_half[:], op=ALU.pow)
 
-        def leave_psum(i):
-            scaled[i] = work.tile([P, HEADS, D], F32, name="scaled")
-            sum_sq[i] = stats.tile([P, HEADS], F32, name="sum_sq")
-            apply_gain(i, 0)
-            sum_squares(i, 1)
-            sum_squares(i, 0)
-            apply_gain(i, 1)
-            total = stats.tile([P, 1], F32, name="total")
-            nc.gpsimd.tensor_scalar(
-                out=total[:],
-                in0=sum_sq[i][:, 0:1],
-                scalar1=sum_sq[i][:, 1:2],
-                scalar2=E * EPS,
-                op0=ALU.add,
-                op1=ALU.add,
-            )
-            inv_rms[i] = stats.tile([P, 1], F32, name="inv_rms")
-            nc.gpsimd.tensor_tensor(out=inv_rms[i][:], in0=total[:], in1=minus_half[:], op=ALU.pow)
-
-        def finish(i):
-            row = scaled[i][:].rearrange("p h d -> p (h d)")
+        def finish(i, h):
+            n, t = i // BLOCK_TILES, i % BLOCK_TILES
             nc.vector.scalar_tensor_tensor(
-                out=row,
-                in0=row,
+                out=scaled[i][:, h, :],
+                in0=scaled[i][:, h, :],
                 scalar=inv_rms[i][:, 0:1],
-                in1=x_sb[i // BLOCK_TILES][:, i % BLOCK_TILES, :],
+                in1=x_sb[n][:, t, h * D : (h + 1) * D],
                 op0=ALU.mult,
                 op1=ALU.add,
             )
-            nc.sync.dma_start(out=out_blocks[i // BLOCK_TILES][:, i % BLOCK_TILES, :], in_=row)
+            if h == HEADS - 1:
+                nc.sync.dma_start(out=out_blocks[n][:, t, :], in_=scaled[i][:].rearrange("p h d -> p (h d)"))
 
-        for i in range(-1, N_TILES + 5):
-            if live(i) and i % BLOCK_TILES == 0:
+        turn_keys(0)
+        for j in range(-2, HEADS * N_TILES + 14):
+            i, h = at(j, 0)
+
+            if live(i) and j % (HEADS * BLOCK_TILES) == 0:
                 n = i // BLOCK_TILES
                 if n + 2 < N_BLOCKS:
                     nc.sync.dma_start(out=q_sb[n + 2][:], in_=q_blocks[n + 2])
                 if n + 1 < N_BLOCKS:
                     nc.sync.dma_start(out=x_sb[n + 1][:], in_=x_blocks[n + 1])
-            if live(i - 4):
-                leave_psum(i - 4)
+
             for c in range(D_CHUNKS):
                 if live(i):
-                    score(i, 0, c)
-                if live(i + 1):
-                    turn_q(i + 1, 2 * c)
-                    turn_q(i + 1, 2 * c + 1)
-            for c in range(D_CHUNKS):
-                if live(i):
-                    score(i, 1, c)
-                if live(i - 2) and c < HEADS:
-                    turn_e(i - 2, c, 0)
-                    turn_e(i - 2, c, 1)
-            for h in range(HEADS):
-                if live(i - 3):
-                    retrieve(i - 3, h)
-            if live(i + 1):
-                keep_qT(i + 1)
-            if live(i):
-                softmax_numerator(i, 0)
-            if live(i - 5):
-                finish(i - 5)
-            if live(i - 2):
-                group_e(i - 2)
-            if live(i):
-                softmax_numerator(i, 1)
-            if live(i - 2):
+                    score(i, h, c)
+                if c < GAPS and h == 0 and live(i + 1):
+                    for piece in range(c, HEADS * D_CHUNKS, GAPS):
+                        turn_q(i + 1, piece)
+                if c < GAPS and h == 1 and live(i - 2):
+                    for piece in range(c, HEADS * PAIRS, GAPS):
+                        turn_e(i - 2, piece // PAIRS, piece % PAIRS)
+            if live(at(j, 8)[0]):
+                retrieve(*at(j, 8))
+
+            if live(at(j, 1)[0]):
+                row_max(*at(j, 1))
+            if live(at(j, 9)[0]):
+                apply_gain(*at(j, 9))
+            if live(at(j, 13)[0]):
+                finish(*at(j, 13))
+            if h == 0 and live(i - 2):
                 invert_row_sum(i - 2)
-                quantise_e(i - 2)
+            if h == 1 and live(i - 3):
+                quantise_e(i - 3)
+
+            if live(at(j, 2)[0]):
+                exponentials(*at(j, 2))
+            if live(at(j, 10)[0]):
+                sum_squares(*at(j, 10))
+            if h == 1 and live(i + 1):
+                keep_qT(i + 1)
+            if h == 0 and live(i - 3):
+                group_e(i - 3)
+
+            if j == -1:
+                turn_keys(1)

@@ -179,13 +179,17 @@ def tile_hopfieldmemorylayer_pb_t_e_kernel(
 
         def group_e(i):
             grouped[i] = work.tile([P, HEADS, P, PACK], BF16, name="grouped", align_bytes=64)
-            nc.scalar.copy(
-                out=grouped[i][:]
+            side_by_side = (
+                grouped[i][:]
                 .rearrange("p h r t -> p (h r t)")
                 .bitcast(F32)
-                .rearrange("p (h r u) -> p h r u", h=HEADS, u=PAIRS),
-                in_=eT_ps[i][:].rearrange("p h u r -> p h r u"),
+                .rearrange("p (h r u) -> p h r u", h=HEADS, u=PAIRS)
             )
+            as_turned = eT_ps[i][:].rearrange("p h u r -> p h r u")
+            if i % 2 == 0:
+                nc.vector.tensor_copy(out=side_by_side, in_=as_turned)
+            else:
+                nc.scalar.copy(out=side_by_side, in_=as_turned)
 
         def quantise_e(i):
             e_codes[i] = work.tile([P, HEADS * P], U32, name="e_codes", align_bytes=64)
@@ -249,18 +253,39 @@ def tile_hopfieldmemorylayer_pb_t_e_kernel(
                 inv_rms[i] = stats.tile([P, 1], F32, name="inv_rms")
                 nc.gpsimd.tensor_tensor(out=inv_rms[i][:], in0=total[:], in1=minus_half[:], op=ALU.pow)
 
-        def finish(i, h):
-            n, t = i // BLOCK_TILES, i % BLOCK_TILES
+        def residual(i, h):
+            return x_sb[i // BLOCK_TILES][:, i % BLOCK_TILES, h * D : (h + 1) * D]
+
+        def finish_on_vector(i, h):
             nc.vector.scalar_tensor_tensor(
                 out=scaled[i][:, h, :],
                 in0=scaled[i][:, h, :],
                 scalar=inv_rms[i][:, 0:1],
-                in1=x_sb[n][:, t, h * D : (h + 1) * D],
+                in1=residual(i, h),
                 op0=ALU.mult,
                 op1=ALU.add,
             )
-            if h == HEADS - 1:
-                nc.sync.dma_start(out=out_blocks[n][:, t, :], in_=scaled[i][:].rearrange("p h d -> p (h d)"))
+
+        def finish_on_gpsimd(i):
+            for h in range(HEADS):
+                nc.gpsimd.tensor_scalar(
+                    out=scaled[i][:, h, :],
+                    in0=scaled[i][:, h, :],
+                    scalar1=inv_rms[i][:, 0:1],
+                    scalar2=0.0,
+                    op0=ALU.mult,
+                    op1=ALU.add,
+                )
+            for h in range(HEADS):
+                nc.gpsimd.tensor_tensor(
+                    out=scaled[i][:, h, :], in0=scaled[i][:, h, :], in1=residual(i, h), op=ALU.add
+                )
+
+        def store(i):
+            nc.sync.dma_start(
+                out=out_blocks[i // BLOCK_TILES][:, i % BLOCK_TILES, :],
+                in_=scaled[i][:].rearrange("p h d -> p (h d)"),
+            )
 
         turn_keys(0)
         for j in range(-2, HEADS * N_TILES + 14):
@@ -289,8 +314,14 @@ def tile_hopfieldmemorylayer_pb_t_e_kernel(
                 row_max(*at(j, 1))
             if live(at(j, 9)[0]):
                 apply_gain(*at(j, 9))
-            if live(at(j, 13)[0]):
-                finish(*at(j, 13))
+            last_i, last_h = at(j, 13)
+            if live(last_i) and last_i % 2 == 0 and last_h == 0:
+                finish_on_gpsimd(last_i)
+                store(last_i)
+            if live(last_i) and last_i % 2 == 1:
+                finish_on_vector(last_i, last_h)
+                if last_h == HEADS - 1:
+                    store(last_i)
             if h == 0 and live(i - 2):
                 invert_row_sum(i - 2)
             if h == 1 and live(i - 3):

@@ -55,6 +55,8 @@ def tile_hopfieldmemorylayer_pb_t_e_kernel(
         nc.vector.memset(v_planes[:].bitcast(I32), 0)
         minus_half = keep.tile([P, 1], F32)
         nc.vector.memset(minus_half[:], -0.5)
+        minus_one = keep.tile([P, HEADS], F32)
+        nc.vector.memset(minus_one[:], -1.0)
         ident_bf = keep.tile([P, P], BF16)
         masks.make_identity(nc, ident_bf[:])
         ident_f32 = keep.tile([P, P], F32)
@@ -179,17 +181,13 @@ def tile_hopfieldmemorylayer_pb_t_e_kernel(
 
         def group_e(i):
             grouped[i] = work.tile([P, HEADS, P, PACK], BF16, name="grouped", align_bytes=64)
-            side_by_side = (
-                grouped[i][:]
+            nc.scalar.copy(
+                out=grouped[i][:]
                 .rearrange("p h r t -> p (h r t)")
                 .bitcast(F32)
-                .rearrange("p (h r u) -> p h r u", h=HEADS, u=PAIRS)
+                .rearrange("p (h r u) -> p h r u", h=HEADS, u=PAIRS),
+                in_=eT_ps[i][:].rearrange("p h u r -> p h r u"),
             )
-            as_turned = eT_ps[i][:].rearrange("p h u r -> p h r u")
-            if i % 2 == 0:
-                nc.vector.tensor_copy(out=side_by_side, in_=as_turned)
-            else:
-                nc.scalar.copy(out=side_by_side, in_=as_turned)
 
         def quantise_e(i):
             e_codes[i] = work.tile([P, HEADS * P], U32, name="e_codes", align_bytes=64)
@@ -202,7 +200,7 @@ def tile_hopfieldmemorylayer_pb_t_e_kernel(
 
         def invert_row_sum(i):
             inv_sum[i] = stats.tile([P, HEADS], F32, name="inv_sum")
-            nc.vector.reciprocal(out=inv_sum[i][:], in_=row_sum[i][:])
+            nc.gpsimd.tensor_tensor(out=inv_sum[i][:], in0=row_sum[i][:], in1=minus_one[:], op=ALU.pow)
 
         def retrieve(i, h):
             acc[i, h] = psum_acc.tile([P, D], F32, name="acc")
@@ -253,42 +251,21 @@ def tile_hopfieldmemorylayer_pb_t_e_kernel(
                 inv_rms[i] = stats.tile([P, 1], F32, name="inv_rms")
                 nc.gpsimd.tensor_tensor(out=inv_rms[i][:], in0=total[:], in1=minus_half[:], op=ALU.pow)
 
-        def residual(i, h):
-            return x_sb[i // BLOCK_TILES][:, i % BLOCK_TILES, h * D : (h + 1) * D]
-
-        def finish_on_vector(i, h):
+        def finish(i):
+            n, t = i // BLOCK_TILES, i % BLOCK_TILES
+            row = scaled[i][:].rearrange("p h d -> p (h d)")
             nc.vector.scalar_tensor_tensor(
-                out=scaled[i][:, h, :],
-                in0=scaled[i][:, h, :],
+                out=row,
+                in0=row,
                 scalar=inv_rms[i][:, 0:1],
-                in1=residual(i, h),
+                in1=x_sb[n][:, t, :],
                 op0=ALU.mult,
                 op1=ALU.add,
             )
-
-        def finish_on_gpsimd(i):
-            for h in range(HEADS):
-                nc.gpsimd.tensor_scalar(
-                    out=scaled[i][:, h, :],
-                    in0=scaled[i][:, h, :],
-                    scalar1=inv_rms[i][:, 0:1],
-                    scalar2=0.0,
-                    op0=ALU.mult,
-                    op1=ALU.add,
-                )
-            for h in range(HEADS):
-                nc.gpsimd.tensor_tensor(
-                    out=scaled[i][:, h, :], in0=scaled[i][:, h, :], in1=residual(i, h), op=ALU.add
-                )
-
-        def store(i):
-            nc.sync.dma_start(
-                out=out_blocks[i // BLOCK_TILES][:, i % BLOCK_TILES, :],
-                in_=scaled[i][:].rearrange("p h d -> p (h d)"),
-            )
+            nc.sync.dma_start(out=out_blocks[n][:, t, :], in_=row)
 
         turn_keys(0)
-        for j in range(-2, HEADS * N_TILES + 14):
+        for j in range(-2, HEADS * (N_TILES + 7) + 1):
             i, h = at(j, 0)
 
             if live(i) and j % (HEADS * BLOCK_TILES) == 0:
@@ -314,18 +291,13 @@ def tile_hopfieldmemorylayer_pb_t_e_kernel(
                 row_max(*at(j, 1))
             if live(at(j, 9)[0]):
                 apply_gain(*at(j, 9))
-            last_i, last_h = at(j, 13)
-            if live(last_i) and last_i % 2 == 0 and last_h == 0:
-                finish_on_gpsimd(last_i)
-                store(last_i)
-            if live(last_i) and last_i % 2 == 1:
-                finish_on_vector(last_i, last_h)
-                if last_h == HEADS - 1:
-                    store(last_i)
-            if h == 0 and live(i - 2):
-                invert_row_sum(i - 2)
+            if h == 0 and live(i - 7):
+                finish(i - 7)
             if h == 1 and live(i - 3):
                 quantise_e(i - 3)
+
+            if h == 0 and live(i - 2):
+                invert_row_sum(i - 2)
 
             if live(at(j, 2)[0]):
                 exponentials(*at(j, 2))

@@ -27,6 +27,7 @@ BLOCK_TILES = 4
 N_BLOCKS = ROWS // (P * BLOCK_TILES)
 N_TILES = ROWS // P
 GAPS = D_CHUNKS - 1
+WORD_BLOCKS = D // (2 * P)
 
 FLOPS = 2 * 2 * ROWS * HEADS * D * SLOTS
 
@@ -57,8 +58,6 @@ def tile_hopfieldmemorylayer_pb_t_e_kernel(
         nc.vector.memset(minus_half[:], -0.5)
         minus_one = keep.tile([P, HEADS], F32)
         nc.vector.memset(minus_one[:], -1.0)
-        ident_bf = keep.tile([P, P], BF16)
-        masks.make_identity(nc, ident_bf[:])
         ident_f32 = keep.tile([P, P], F32)
         masks.make_identity(nc, ident_f32[:])
         table_warmer = keep.tile([P, 1], F32)
@@ -104,23 +103,23 @@ def tile_hopfieldmemorylayer_pb_t_e_kernel(
         kT = keep.tile([P, HEADS, D_CHUNKS, SLOTS], BF16)
 
         def turn_keys(h):
-            for half in range(2):
-                kT_ps = psum_scores.tile([P, 2, PACK, P], BF16, tag="s_ps")
-                for j in range(2):
-                    c = 2 * half + j
-                    for a in range(PACK):
-                        nc.tensor.transpose(
-                            kT_ps[:, j, a, :], k_sb[:, h, a, c * P : (c + 1) * P], ident_bf[:]
-                        )
+            for b in range(WORD_BLOCKS):
+                kT_ps = psum_scores.tile([P, PACK, P], F32, tag="s_ps")
+                for a in range(PACK):
+                    words = k_sb[:, h, a, :].bitcast(F32)
+                    nc.tensor.transpose(kT_ps[:, a, :], words[:, b * P : (b + 1) * P], ident_f32[:])
                 in_order = "d (u p i) -> d u p i"
-                as_turned = "d (u i) p -> d u p i"
+                as_turned = (
+                    kT_ps[:]
+                    .rearrange("d a p -> d (a p)")
+                    .bitcast(BF16)
+                    .rearrange("d (u i p e) -> d e u p i", u=PAIRS, i=2, e=2)
+                )
                 nc.vector.tensor_copy(
-                    out=kT[:, h, 2 * half, :].rearrange(in_order, u=PAIRS, i=2),
-                    in_=kT_ps[:, 0].rearrange(as_turned, i=2),
+                    out=kT[:, h, 2 * b, :].rearrange(in_order, u=PAIRS, i=2), in_=as_turned[:, 0]
                 )
                 nc.scalar.copy(
-                    out=kT[:, h, 2 * half + 1, :].rearrange(in_order, u=PAIRS, i=2),
-                    in_=kT_ps[:, 1].rearrange(as_turned, i=2),
+                    out=kT[:, h, 2 * b + 1, :].rearrange(in_order, u=PAIRS, i=2), in_=as_turned[:, 1]
                 )
 
         qT_ps, qT, s_ps, neg_max, row_sum, e_sb, eT_ps = {}, {}, {}, {}, {}, {}, {}
@@ -134,20 +133,23 @@ def tile_hopfieldmemorylayer_pb_t_e_kernel(
 
         def turn_q(i, j):
             if j == 0:
-                qT_ps[i] = psum_turn.tile([P, HEADS * D_CHUNKS, P], BF16, name="qT_ps")
-            rows = q_sb[i // BLOCK_TILES][:, i % BLOCK_TILES, :]
-            nc.tensor.transpose(qT_ps[i][:, j, :], rows[:, j * P : (j + 1) * P], ident_bf[:])
+                qT_ps[i] = psum_turn.tile([P, HEADS * WORD_BLOCKS, P], F32, name="qT_ps")
+            words = q_sb[i // BLOCK_TILES][:, i % BLOCK_TILES, :].bitcast(F32)
+            nc.tensor.transpose(qT_ps[i][:, j, :], words[:, j * P : (j + 1) * P], ident_f32[:])
 
         def keep_qT(i):
-            qT[i] = work.tile([P, HEADS * D_CHUNKS, P], BF16, name="qT")
-            nc.scalar.copy(out=qT[i][:], in_=qT_ps[i][:])
+            qT[i] = work.tile([P, HEADS * WORD_BLOCKS, P, 2], BF16, name="qT")
+            nc.scalar.copy(
+                out=qT[i][:].rearrange("p j r e -> p (j r e)").bitcast(F32),
+                in_=qT_ps[i][:].rearrange("p j r -> p (j r)"),
+            )
 
         def score(i, h, c):
             if c == 0:
                 s_ps[i, h] = psum_scores.tile([P, SLOTS], F32, name="s_ps")
             nc.tensor.matmul(
                 s_ps[i, h][:],
-                lhsT=qT[i][:, D_CHUNKS * h + c, :],
+                lhsT=qT[i][:, WORD_BLOCKS * h + c // 2, :, c % 2],
                 rhs=kT[:, h, c, :],
                 start=(c == 0),
                 stop=(c == D_CHUNKS - 1),
@@ -279,7 +281,7 @@ def tile_hopfieldmemorylayer_pb_t_e_kernel(
                 if live(i):
                     score(i, h, c)
                 if c < GAPS and h == 0 and live(i + 1):
-                    for piece in range(c, HEADS * D_CHUNKS, GAPS):
+                    for piece in range(c, HEADS * WORD_BLOCKS, GAPS):
                         turn_q(i + 1, piece)
                 if c < GAPS and h == 1 and live(i - 2):
                     for piece in range(c, HEADS * PAIRS, GAPS):

@@ -27,6 +27,8 @@ BLOCK_TILES = 4
 N_BLOCKS = ROWS // (P * BLOCK_TILES)
 N_TILES = ROWS // P
 GAPS = D_CHUNKS - 1
+EARLY_FINISH = 5
+LATE_FINISH = 7
 WORD_BLOCKS = D // (2 * P)
 
 FLOPS = 2 * 2 * ROWS * HEADS * D * SLOTS
@@ -70,10 +72,13 @@ def tile_hopfieldmemorylayer_pb_t_e_kernel(
             x_sb.append(keep.tile([P, BLOCK_TILES, E], BF16, name="x_sb%d" % n))
         k_sb = keep.tile([P, HEADS, PACK, D], BF16)
         k_by_slot_group = k.rearrange("h (p a) d -> h p a d", a=PACK)
-        nc.sync.dma_start(out=k_sb[:, 0], in_=k_by_slot_group[0])
         nc.sync.dma_start(out=q_sb[0][:, 0:1], in_=q_blocks[0][:, 0:1])
+        for b in range(WORD_BLOCKS):
+            features = slice(2 * P * b, 2 * P * (b + 1))
+            nc.sync.dma_start(out=k_sb[:, 0, :, features], in_=k_by_slot_group[0][:, :, features])
         nc.sync.dma_start(out=k_sb[:, 1], in_=k_by_slot_group[1])
-        nc.sync.dma_start(out=q_sb[0][:, 1:], in_=q_blocks[0][:, 1:])
+        nc.sync.dma_start(out=q_sb[0][:, 1:2], in_=q_blocks[0][:, 1:2])
+        nc.sync.dma_start(out=q_sb[0][:, 2:], in_=q_blocks[0][:, 2:])
         v_codes = keep.tile([P, HEADS, D], U32, align_bytes=64)
         nc.sync.dma_start(
             out=v_codes[:].bitcast(I32),
@@ -115,18 +120,21 @@ def tile_hopfieldmemorylayer_pb_t_e_kernel(
                     .bitcast(BF16)
                     .rearrange("d (u i p e) -> d e u p i", u=PAIRS, i=2, e=2)
                 )
-                nc.vector.tensor_copy(
-                    out=kT[:, h, 2 * b, :].rearrange(in_order, u=PAIRS, i=2), in_=as_turned[:, 0]
-                )
-                nc.scalar.copy(
-                    out=kT[:, h, 2 * b + 1, :].rearrange(in_order, u=PAIRS, i=2), in_=as_turned[:, 1]
-                )
+                for e in range(2):
+                    chunk = kT[:, h, 2 * b + e, :].rearrange(in_order, u=PAIRS, i=2)
+                    if b == 0:
+                        nc.vector.tensor_copy(out=chunk, in_=as_turned[:, e])
+                    else:
+                        nc.scalar.copy(out=chunk, in_=as_turned[:, e])
 
         qT_ps, qT, s_ps, neg_max, row_sum, e_sb, eT_ps = {}, {}, {}, {}, {}, {}, {}
         grouped, e_codes, e_scales, inv_sum, acc, sum_sq, scaled, inv_rms = {}, {}, {}, {}, {}, {}, {}, {}
 
         def live(i):
             return 0 <= i < N_TILES
+
+        def finish_lag(i):
+            return EARLY_FINISH if i < N_TILES // 2 else LATE_FINISH
 
         def at(j, lag):
             return (j - lag) // HEADS, (j - lag) % HEADS
@@ -266,8 +274,7 @@ def tile_hopfieldmemorylayer_pb_t_e_kernel(
             )
             nc.sync.dma_start(out=out_blocks[n][:, t, :], in_=row)
 
-        turn_keys(0)
-        for j in range(-2, HEADS * (N_TILES + 7) + 1):
+        for j in range(-3, HEADS * (N_TILES + LATE_FINISH) + 2):
             i, h = at(j, 0)
 
             if live(i) and j % (HEADS * BLOCK_TILES) == 0:
@@ -280,22 +287,23 @@ def tile_hopfieldmemorylayer_pb_t_e_kernel(
             for c in range(D_CHUNKS):
                 if live(i):
                     score(i, h, c)
-                if c < GAPS and h == 0 and live(i + 1):
+                if c < GAPS and h == 1 and live(i + 2):
                     for piece in range(c, HEADS * WORD_BLOCKS, GAPS):
-                        turn_q(i + 1, piece)
-                if c < GAPS and h == 1 and live(i - 2):
+                        turn_q(i + 2, piece)
+                if c < GAPS and h == 0 and live(i - 2):
                     for piece in range(c, HEADS * PAIRS, GAPS):
                         turn_e(i - 2, piece // PAIRS, piece % PAIRS)
-            if live(at(j, 8)[0]):
-                retrieve(*at(j, 8))
+            if live(at(j, 7)[0]):
+                retrieve(*at(j, 7))
 
             if live(at(j, 1)[0]):
                 row_max(*at(j, 1))
-            if live(at(j, 9)[0]):
-                apply_gain(*at(j, 9))
-            if h == 0 and live(i - 7):
-                finish(i - 7)
-            if h == 1 and live(i - 3):
+            if live(at(j, 8)[0]):
+                apply_gain(*at(j, 8))
+            for lag in (EARLY_FINISH, LATE_FINISH):
+                if h == 1 and live(i - lag) and finish_lag(i - lag) == lag:
+                    finish(i - lag)
+            if h == 0 and live(i - 3):
                 quantise_e(i - 3)
 
             if h == 0 and live(i - 2):
@@ -303,12 +311,13 @@ def tile_hopfieldmemorylayer_pb_t_e_kernel(
 
             if live(at(j, 2)[0]):
                 exponentials(*at(j, 2))
-            if live(at(j, 10)[0]):
-                sum_squares(*at(j, 10))
-            if h == 1 and live(i + 1):
+            if live(at(j, 9)[0]):
+                sum_squares(*at(j, 9))
+            if h == 0 and live(i + 1):
                 keep_qT(i + 1)
-            if h == 0 and live(i - 3):
-                group_e(i - 3)
+            if h == 1 and live(i - 2):
+                group_e(i - 2)
 
-            if j == -1:
+            if j == -2:
+                turn_keys(0)
                 turn_keys(1)

@@ -274,7 +274,7 @@ def tile_hopfieldmemorylayer_pb_t_e_kernel(
             )
             nc.sync.dma_start(out=out_blocks[n][:, t, :], in_=row)
 
-        for j in range(-3, HEADS * (N_TILES + LATE_FINISH) + 2):
+        for j in range(-2, HEADS * (N_TILES + LATE_FINISH) + 2):
             i, h = at(j, 0)
 
             if live(i) and j % (HEADS * BLOCK_TILES) == 0:
@@ -284,40 +284,41 @@ def tile_hopfieldmemorylayer_pb_t_e_kernel(
                 if n + 1 < N_BLOCKS:
                     nc.sync.dma_start(out=x_sb[n + 1][:], in_=x_blocks[n + 1])
 
+            if live(at(j, 2)[0]):
+                exponentials(*at(j, 2))
+
             for c in range(D_CHUNKS):
                 if live(i):
                     score(i, h, c)
-                if c < GAPS and h == 1 and live(i + 2):
+                if c < GAPS and h == 0 and live(i + 1):
                     for piece in range(c, HEADS * WORD_BLOCKS, GAPS):
-                        turn_q(i + 2, piece)
-                if c < GAPS and h == 0 and live(i - 2):
-                    for piece in range(c, HEADS * PAIRS, GAPS):
-                        turn_e(i - 2, piece // PAIRS, piece % PAIRS)
-            if live(at(j, 7)[0]):
-                retrieve(*at(j, 7))
+                        turn_q(i + 1, piece)
+                if c in (0, GAPS - 1) and h == 1 and live(i - 1):
+                    for u in range(PAIRS):
+                        turn_e(i - 1, c // (GAPS - 1), u)
+            if live(at(j, 6)[0]):
+                retrieve(*at(j, 6))
 
             if live(at(j, 1)[0]):
                 row_max(*at(j, 1))
-            if live(at(j, 8)[0]):
-                apply_gain(*at(j, 8))
+            if live(at(j, 7)[0]):
+                apply_gain(*at(j, 7))
             for lag in (EARLY_FINISH, LATE_FINISH):
-                if h == 1 and live(i - lag) and finish_lag(i - lag) == lag:
+                if h == 0 and live(i - lag) and finish_lag(i - lag) == lag:
                     finish(i - lag)
-            if h == 0 and live(i - 3):
-                quantise_e(i - 3)
+            if h == 1 and live(i - 2):
+                quantise_e(i - 2)
 
             if h == 0 and live(i - 2):
                 invert_row_sum(i - 2)
 
-            if live(at(j, 2)[0]):
-                exponentials(*at(j, 2))
-            if live(at(j, 9)[0]):
-                sum_squares(*at(j, 9))
-            if h == 0 and live(i + 1):
+            if live(at(j, 8)[0]):
+                sum_squares(*at(j, 8))
+            if h == 1 and live(i + 1):
                 keep_qT(i + 1)
-            if h == 1 and live(i - 2):
+            if h == 0 and live(i - 2):
                 group_e(i - 2)
 
-            if j == -2:
+            if j == -1:
                 turn_keys(0)
                 turn_keys(1)

@@ -27,6 +27,7 @@ BLOCK_TILES = 4
 N_BLOCKS = ROWS // (P * BLOCK_TILES)
 N_TILES = ROWS // P
 GAPS = D_CHUNKS - 1
+WARM_UP = 4
 EARLY_FINISH = 5
 LATE_FINISH = 7
 WORD_BLOCKS = D // (2 * P)
@@ -54,6 +55,15 @@ def tile_hopfieldmemorylayer_pb_t_e_kernel(
         psum_acc = ctx.enter_context(tc.psum_pool(name="psum_acc", bufs=3))
         ctx.enter_context(tc.manual_schedule())
 
+        zeros = keep.tile([P, SLOTS], BF16)
+        nc.vector.memset(zeros[:], 0.0)
+
+        def keep_warm(times):
+            for turn in range(times):
+                idle_ps = psum_acc.tile([P, SLOTS], F32, tag="acc")
+                nc.tensor.matmul(idle_ps[:], lhsT=zeros[:, 0:P], rhs=zeros[:], start=True, stop=True)
+
+        keep_warm(WARM_UP)
         v_planes = keep.tile([P, HEADS, D], U8, align_bytes=64)
         nc.vector.memset(v_planes[:].bitcast(I32), 0)
         minus_half = keep.tile([P, 1], F32)
@@ -113,6 +123,7 @@ def tile_hopfieldmemorylayer_pb_t_e_kernel(
                 for a in range(PACK):
                     words = k_sb[:, h, a, :].bitcast(F32)
                     nc.tensor.transpose(kT_ps[:, a, :], words[:, b * P : (b + 1) * P], ident_f32[:])
+                keep_warm(1)
                 in_order = "d (u p i) -> d u p i"
                 as_turned = (
                     kT_ps[:]

@@ -301,12 +301,12 @@ def tile_hopfieldmemorylayer_pb_t_e_kernel(
             for c in range(D_CHUNKS):
                 if live(i):
                     score(i, h, c)
-                if c < GAPS and h == 0 and live(i + 1):
-                    for piece in range(c, HEADS * WORD_BLOCKS, GAPS):
+                if c == GAPS - 1 and h == 0 and live(i + 1):
+                    for piece in range(HEADS * WORD_BLOCKS):
                         turn_q(i + 1, piece)
-                if c in (0, GAPS - 1) and h == 1 and live(i - 1):
-                    for u in range(PAIRS):
-                        turn_e(i - 1, c // (GAPS - 1), u)
+                if c == GAPS - 1 and h == 1 and live(i - 1):
+                    for piece in range(HEADS * PAIRS):
+                        turn_e(i - 1, piece // PAIRS, piece % PAIRS)
             if live(at(j, 6)[0]):
                 retrieve(*at(j, 6))
 

@@ -29,7 +29,7 @@ N_TILES = ROWS // P
 GAPS = D_CHUNKS - 1
 WARM_UP = 4
 EARLY_FINISH = 5
-LATE_FINISH = 7
+LATE_FINISH = 6
 WORD_BLOCKS = D // (2 * P)
 
 FLOPS = 2 * 2 * ROWS * HEADS * D * SLOTS
@@ -117,26 +117,27 @@ def tile_hopfieldmemorylayer_pb_t_e_kernel(
 
         kT = keep.tile([P, HEADS, D_CHUNKS, SLOTS], BF16)
 
-        def turn_keys(h):
-            for b in range(WORD_BLOCKS):
+        def turn_keys(h, b):
+            if h == 0:
                 kT_ps = psum_scores.tile([P, PACK, P], F32, tag="s_ps")
-                for a in range(PACK):
-                    words = k_sb[:, h, a, :].bitcast(F32)
-                    nc.tensor.transpose(kT_ps[:, a, :], words[:, b * P : (b + 1) * P], ident_f32[:])
-                keep_warm(1)
-                in_order = "d (u p i) -> d u p i"
-                as_turned = (
-                    kT_ps[:]
-                    .rearrange("d a p -> d (a p)")
-                    .bitcast(BF16)
-                    .rearrange("d (u i p e) -> d e u p i", u=PAIRS, i=2, e=2)
-                )
-                for e in range(2):
-                    chunk = kT[:, h, 2 * b + e, :].rearrange(in_order, u=PAIRS, i=2)
-                    if b == 0:
-                        nc.vector.tensor_copy(out=chunk, in_=as_turned[:, e])
-                    else:
-                        nc.scalar.copy(out=chunk, in_=as_turned[:, e])
+            else:
+                kT_ps = psum_acc.tile([P, PACK, P], F32, tag="acc")
+            for a in range(PACK):
+                words = k_sb[:, h, a, :].bitcast(F32)
+                nc.tensor.transpose(kT_ps[:, a, :], words[:, b * P : (b + 1) * P], ident_f32[:])
+            in_order = "d (u p i) -> d u p i"
+            as_turned = (
+                kT_ps[:]
+                .rearrange("d a p -> d (a p)")
+                .bitcast(BF16)
+                .rearrange("d (u i p e) -> d e u p i", u=PAIRS, i=2, e=2)
+            )
+            for e in range(2):
+                chunk = kT[:, h, 2 * b + e, :].rearrange(in_order, u=PAIRS, i=2)
+                if b == 0:
+                    nc.vector.tensor_copy(out=chunk, in_=as_turned[:, e])
+                else:
+                    nc.scalar.copy(out=chunk, in_=as_turned[:, e])
 
         qT_ps, qT, s_ps, neg_max, row_sum, e_sb, eT_ps = {}, {}, {}, {}, {}, {}, {}
         grouped, e_codes, e_scales, inv_sum, acc, sum_sq, scaled, inv_rms = {}, {}, {}, {}, {}, {}, {}, {}
@@ -301,6 +302,8 @@ def tile_hopfieldmemorylayer_pb_t_e_kernel(
             for c in range(D_CHUNKS):
                 if live(i):
                     score(i, h, c)
+                if j == 0 and c < WORD_BLOCKS:
+                    turn_keys(1, c)
                 if c == GAPS - 1 and h == 0 and live(i + 1):
                     for piece in range(HEADS * WORD_BLOCKS):
                         turn_q(i + 1, piece)
@@ -331,5 +334,6 @@ def tile_hopfieldmemorylayer_pb_t_e_kernel(
                 group_e(i - 2)
 
             if j == -1:
-                turn_keys(0)
-                turn_keys(1)
+                for b in range(WORD_BLOCKS):
+                    turn_keys(0, b)
+                    keep_warm(1)

@@ -28,8 +28,8 @@ N_BLOCKS = ROWS // (P * BLOCK_TILES)
 N_TILES = ROWS // P
 GAPS = D_CHUNKS - 1
 WARM_UP = 4
-EARLY_FINISH = 5
-LATE_FINISH = 6
+EARLY_FINISH = 4
+LATE_FINISH = 5
 WORD_BLOCKS = D // (2 * P)
 
 FLOPS = 2 * 2 * ROWS * HEADS * D * SLOTS
@@ -310,28 +310,28 @@ def tile_hopfieldmemorylayer_pb_t_e_kernel(
                 if c == GAPS - 1 and h == 1 and live(i - 1):
                     for piece in range(HEADS * PAIRS):
                         turn_e(i - 1, piece // PAIRS, piece % PAIRS)
-            if live(at(j, 6)[0]):
-                retrieve(*at(j, 6))
+            if live(at(j, 5)[0]):
+                retrieve(*at(j, 5))
 
             if live(at(j, 1)[0]):
                 row_max(*at(j, 1))
-            if live(at(j, 7)[0]):
-                apply_gain(*at(j, 7))
+            if live(at(j, 6)[0]):
+                apply_gain(*at(j, 6))
             for lag in (EARLY_FINISH, LATE_FINISH):
-                if h == 0 and live(i - lag) and finish_lag(i - lag) == lag:
+                if h == 1 and live(i - lag) and finish_lag(i - lag) == lag:
                     finish(i - lag)
-            if h == 1 and live(i - 2):
+            if h == 0 and live(i - 2):
                 quantise_e(i - 2)
 
             if h == 0 and live(i - 2):
                 invert_row_sum(i - 2)
 
-            if live(at(j, 8)[0]):
-                sum_squares(*at(j, 8))
+            if live(at(j, 7)[0]):
+                sum_squares(*at(j, 7))
             if h == 1 and live(i + 1):
                 keep_qT(i + 1)
-            if h == 0 and live(i - 2):
-                group_e(i - 2)
+            if h == 1 and live(i - 1):
+                group_e(i - 1)
 
             if j == -1:
                 for b in range(WORD_BLOCKS):

@@ -83,9 +83,9 @@ def tile_hopfieldmemorylayer_pb_t_e_kernel(
         k_sb = keep.tile([P, HEADS, PACK, D], BF16)
         k_by_slot_group = k.rearrange("h (p a) d -> h p a d", a=PACK)
         nc.sync.dma_start(out=q_sb[0][:, 0:1], in_=q_blocks[0][:, 0:1])
-        for b in range(WORD_BLOCKS):
-            features = slice(2 * P * b, 2 * P * (b + 1))
-            nc.sync.dma_start(out=k_sb[:, 0, :, features], in_=k_by_slot_group[0][:, :, features])
+        for u in range(PAIRS):
+            slots = slice(2 * u, 2 * u + 2)
+            nc.sync.dma_start(out=k_sb[:, 0, slots], in_=k_by_slot_group[0][:, slots])
         nc.sync.dma_start(out=k_sb[:, 1], in_=k_by_slot_group[1])
         nc.sync.dma_start(out=q_sb[0][:, 1:2], in_=q_blocks[0][:, 1:2])
         nc.sync.dma_start(out=q_sb[0][:, 2:], in_=q_blocks[0][:, 2:])
@@ -117,27 +117,21 @@ def tile_hopfieldmemorylayer_pb_t_e_kernel(
 
         kT = keep.tile([P, HEADS, D_CHUNKS, SLOTS], BF16)
 
-        def turn_keys(h, b):
+        def turn_keys(h, u):
             if h == 0:
-                kT_ps = psum_scores.tile([P, PACK, P], F32, tag="s_ps")
+                kT_ps = psum_scores.tile([P, WORD_BLOCKS, 2, P], F32, tag="s_ps")
             else:
-                kT_ps = psum_acc.tile([P, PACK, P], F32, tag="acc")
-            for a in range(PACK):
-                words = k_sb[:, h, a, :].bitcast(F32)
-                nc.tensor.transpose(kT_ps[:, a, :], words[:, b * P : (b + 1) * P], ident_f32[:])
-            in_order = "d (u p i) -> d u p i"
-            as_turned = (
-                kT_ps[:]
-                .rearrange("d a p -> d (a p)")
-                .bitcast(BF16)
-                .rearrange("d (u i p e) -> d e u p i", u=PAIRS, i=2, e=2)
-            )
-            for e in range(2):
-                chunk = kT[:, h, 2 * b + e, :].rearrange(in_order, u=PAIRS, i=2)
-                if b == 0:
-                    nc.vector.tensor_copy(out=chunk, in_=as_turned[:, e])
-                else:
-                    nc.scalar.copy(out=chunk, in_=as_turned[:, e])
+                kT_ps = psum_acc.tile([P, WORD_BLOCKS, 2, P], F32, tag="acc")
+            copy = nc.vector.tensor_copy if u == 0 else nc.scalar.copy
+            for b in range(WORD_BLOCKS):
+                for a in range(2):
+                    words = k_sb[:, h, 2 * u + a, :].bitcast(F32)
+                    nc.tensor.transpose(kT_ps[:, b, a, :], words[:, b * P : (b + 1) * P], ident_f32[:])
+            for b in range(WORD_BLOCKS):
+                copy(
+                    out=kT[:, h, 2 * b : 2 * b + 2, 2 * P * u : 2 * P * (u + 1)].rearrange("d e (p i) -> d e p i", i=2),
+                    in_=kT_ps[:, b].rearrange("d a p -> d (a p)").bitcast(BF16).rearrange("d (i p e) -> d e p i", i=2, e=2),
+                )
 
         qT_ps, qT, s_ps, neg_max, row_sum, e_sb, eT_ps = {}, {}, {}, {}, {}, {}, {}
         grouped, e_codes, e_scales, inv_sum, acc, sum_sq, scaled, inv_rms = {}, {}, {}, {}, {}, {}, {}, {}
@@ -276,15 +270,18 @@ def tile_hopfieldmemorylayer_pb_t_e_kernel(
         def finish(i):
             n, t = i // BLOCK_TILES, i % BLOCK_TILES
             row = scaled[i][:].rearrange("p h d -> p (h d)")
-            nc.vector.scalar_tensor_tensor(
-                out=row,
-                in0=row,
-                scalar=inv_rms[i][:, 0:1],
-                in1=x_sb[n][:, t, :],
-                op0=ALU.mult,
-                op1=ALU.add,
-            )
-            nc.sync.dma_start(out=out_blocks[n][:, t, :], in_=row)
+            width = E // 4 if i == N_TILES - 1 else E
+            for start in range(0, E, width):
+                columns = slice(start, start + width)
+                nc.vector.scalar_tensor_tensor(
+                    out=row[:, columns],
+                    in0=row[:, columns],
+                    scalar=inv_rms[i][:, 0:1],
+                    in1=x_sb[n][:, t, columns],
+                    op0=ALU.mult,
+                    op1=ALU.add,
+                )
+                nc.sync.dma_start(out=out_blocks[n][:, t, columns], in_=row[:, columns])
 
         for j in range(-2, HEADS * (N_TILES + LATE_FINISH) + 2):
             i, h = at(j, 0)
@@ -302,7 +299,7 @@ def tile_hopfieldmemorylayer_pb_t_e_kernel(
             for c in range(D_CHUNKS):
                 if live(i):
                     score(i, h, c)
-                if j == 0 and c < WORD_BLOCKS:
+                if j == 0 and c < PAIRS:
                     turn_keys(1, c)
                 if c == GAPS - 1 and h == 0 and live(i + 1):
                     for piece in range(HEADS * WORD_BLOCKS):
@@ -334,6 +331,6 @@ def tile_hopfieldmemorylayer_pb_t_e_kernel(
                 group_e(i - 1)
 
             if j == -1:
-                for b in range(WORD_BLOCKS):
-                    turn_keys(0, b)
+                for u in range(PAIRS):
+                    turn_keys(0, u)
                     keep_warm(1)

@@ -27,6 +27,7 @@ BLOCK_TILES = 4
 N_BLOCKS = ROWS // (P * BLOCK_TILES)
 N_TILES = ROWS // P
 GAPS = D_CHUNKS - 1
+ON_TENSOR = N_TILES - 6
 WARM_UP = 4
 EARLY_FINISH = 4
 LATE_FINISH = 5
@@ -72,6 +73,8 @@ def tile_hopfieldmemorylayer_pb_t_e_kernel(
         nc.vector.memset(minus_one[:], -1.0)
         ident_f32 = keep.tile([P, P], F32)
         masks.make_identity(nc, ident_f32[:])
+        ident_bf = keep.tile([P, P], BF16)
+        nc.gpsimd.tensor_copy(out=ident_bf[:], in_=ident_f32[:])
         table_warmer = keep.tile([P, 1], F32)
         nc.scalar.activation(out=table_warmer[:], in_=minus_half[:], func=ACT.Exp)
 
@@ -283,6 +286,24 @@ def tile_hopfieldmemorylayer_pb_t_e_kernel(
                 )
                 nc.sync.dma_start(out=out_blocks[n][:, t, columns], in_=row[:, columns])
 
+        spread, finished = {}, {}
+
+        def spread_factor(i):
+            spread[i] = work.tile([P, P], F32, name="spread")
+            nc.scalar.activation(out=spread[i][:], in_=ident_f32[:], func=ACT.Copy, scale=inv_rms[i][:, 0:1])
+
+        def finish_on_tensor(i, h):
+            n, t = i // BLOCK_TILES, i % BLOCK_TILES
+            residual = x_sb[n][:, t, h * D : (h + 1) * D]
+            finished[i, h] = psum_scores.tile([P, D], F32, name="s_ps")
+            nc.tensor.matmul(finished[i, h][:], lhsT=ident_bf[:], rhs=residual, start=True, stop=False)
+            nc.tensor.matmul(finished[i, h][:], lhsT=spread[i][:], rhs=scaled[i][:, h, :], start=False, stop=True)
+
+        def store_finished(i, h):
+            n, t = i // BLOCK_TILES, i % BLOCK_TILES
+            nc.scalar.copy(out=scaled[i][:, h, :], in_=finished[i, h][:])
+            nc.sync.dma_start(out=out_blocks[n][:, t, h * D : (h + 1) * D], in_=scaled[i][:, h, :])
+
         for j in range(-2, HEADS * (N_TILES + LATE_FINISH) + 2):
             i, h = at(j, 0)
 
@@ -310,12 +331,17 @@ def tile_hopfieldmemorylayer_pb_t_e_kernel(
             if live(at(j, 5)[0]):
                 retrieve(*at(j, 5))
 
+            if j == HEADS * N_TILES:
+                spread_factor(ON_TENSOR)
+            if j in (HEADS * N_TILES, HEADS * N_TILES + 1):
+                finish_on_tensor(ON_TENSOR, h)
+
             if live(at(j, 1)[0]):
                 row_max(*at(j, 1))
             if live(at(j, 6)[0]):
                 apply_gain(*at(j, 6))
             for lag in (EARLY_FINISH, LATE_FINISH):
-                if h == 1 and live(i - lag) and finish_lag(i - lag) == lag:
+                if h == 1 and live(i - lag) and finish_lag(i - lag) == lag and i - lag != ON_TENSOR:
                     finish(i - lag)
             if h == 0 and live(i - 2):
                 quantise_e(i - 2)
@@ -329,6 +355,9 @@ def tile_hopfieldmemorylayer_pb_t_e_kernel(
                 keep_qT(i + 1)
             if h == 1 and live(i - 1):
                 group_e(i - 1)
+
+            if j - 1 in (HEADS * N_TILES, HEADS * N_TILES + 1):
+                store_finished(ON_TENSOR, 1 - h)
 
             if j == -1:
                 for u in range(PAIRS):

@@ -316,6 +316,9 @@ def tile_hopfieldmemorylayer_pb_t_e_kernel(
 
             if live(at(j, 2)[0]):
                 exponentials(*at(j, 2))
+            if h == 1 and live(i - 3):
+                for half in range(HEADS):
+                    sum_squares(i - 3, half)
 
             for c in range(D_CHUNKS):
                 if live(i):
@@ -328,8 +331,9 @@ def tile_hopfieldmemorylayer_pb_t_e_kernel(
                 if c == GAPS - 1 and h == 1 and live(i - 1):
                     for piece in range(HEADS * PAIRS):
                         turn_e(i - 1, piece // PAIRS, piece % PAIRS)
-            if live(at(j, 5)[0]):
-                retrieve(*at(j, 5))
+            if h == 1 and live(i - 2):
+                for half in range(HEADS):
+                    retrieve(i - 2, half)
 
             if j == HEADS * N_TILES:
                 spread_factor(ON_TENSOR)
@@ -338,8 +342,9 @@ def tile_hopfieldmemorylayer_pb_t_e_kernel(
 
             if live(at(j, 1)[0]):
                 row_max(*at(j, 1))
-            if live(at(j, 6)[0]):
-                apply_gain(*at(j, 6))
+            if h == 0 and live(i - 3):
+                for half in range(HEADS):
+                    apply_gain(i - 3, half)
             for lag in (EARLY_FINISH, LATE_FINISH):
                 if h == 1 and live(i - lag) and finish_lag(i - lag) == lag and i - lag != ON_TENSOR:
                     finish(i - lag)
@@ -349,15 +354,13 @@ def tile_hopfieldmemorylayer_pb_t_e_kernel(
             if h == 0 and live(i - 2):
                 invert_row_sum(i - 2)
 
-            if live(at(j, 7)[0]):
-                sum_squares(*at(j, 7))
             if h == 1 and live(i + 1):
                 keep_qT(i + 1)
             if h == 1 and live(i - 1):
                 group_e(i - 1)
 
-            if j - 1 in (HEADS * N_TILES, HEADS * N_TILES + 1):
-                store_finished(ON_TENSOR, 1 - h)
+            if j - HEADS in (HEADS * N_TILES, HEADS * N_TILES + 1):
+                store_finished(ON_TENSOR, h)
 
             if j == -1:
                 for u in range(PAIRS):

@@ -86,9 +86,7 @@ def tile_hopfieldmemorylayer_pb_t_e_kernel(
         k_sb = keep.tile([P, HEADS, PACK, D], BF16)
         k_by_slot_group = k.rearrange("h (p a) d -> h p a d", a=PACK)
         nc.sync.dma_start(out=q_sb[0][:, 0:1], in_=q_blocks[0][:, 0:1])
-        for u in range(PAIRS):
-            slots = slice(2 * u, 2 * u + 2)
-            nc.sync.dma_start(out=k_sb[:, 0, slots], in_=k_by_slot_group[0][:, slots])
+        nc.sync.dma_start(out=k_sb[:, 0], in_=k_by_slot_group[0])
         nc.sync.dma_start(out=k_sb[:, 1], in_=k_by_slot_group[1])
         nc.sync.dma_start(out=q_sb[0][:, 1:2], in_=q_blocks[0][:, 1:2])
         nc.sync.dma_start(out=q_sb[0][:, 2:], in_=q_blocks[0][:, 2:])
@@ -120,21 +118,27 @@ def tile_hopfieldmemorylayer_pb_t_e_kernel(
 
         kT = keep.tile([P, HEADS, D_CHUNKS, SLOTS], BF16)
 
-        def turn_keys(h, u):
+        def turn_keys(h, b):
             if h == 0:
-                kT_ps = psum_scores.tile([P, WORD_BLOCKS, 2, P], F32, tag="s_ps")
+                kT_ps = psum_scores.tile([P, PACK, P], F32, tag="s_ps")
             else:
-                kT_ps = psum_acc.tile([P, WORD_BLOCKS, 2, P], F32, tag="acc")
-            copy = nc.vector.tensor_copy if u == 0 else nc.scalar.copy
-            for b in range(WORD_BLOCKS):
-                for a in range(2):
-                    words = k_sb[:, h, 2 * u + a, :].bitcast(F32)
-                    nc.tensor.transpose(kT_ps[:, b, a, :], words[:, b * P : (b + 1) * P], ident_f32[:])
-            for b in range(WORD_BLOCKS):
-                copy(
-                    out=kT[:, h, 2 * b : 2 * b + 2, 2 * P * u : 2 * P * (u + 1)].rearrange("d e (p i) -> d e p i", i=2),
-                    in_=kT_ps[:, b].rearrange("d a p -> d (a p)").bitcast(BF16).rearrange("d (i p e) -> d e p i", i=2, e=2),
-                )
+                kT_ps = psum_acc.tile([P, PACK, P], F32, tag="acc")
+            for a in range(PACK):
+                words = k_sb[:, h, a, :].bitcast(F32)
+                nc.tensor.transpose(kT_ps[:, a, :], words[:, b * P : (b + 1) * P], ident_f32[:])
+            in_order = "d (u p i) -> d u p i"
+            as_turned = (
+                kT_ps[:]
+                .rearrange("d a p -> d (a p)")
+                .bitcast(BF16)
+                .rearrange("d (u i p e) -> d e u p i", u=PAIRS, i=2, e=2)
+            )
+            for e in range(2):
+                chunk = kT[:, h, 2 * b + e, :].rearrange(in_order, u=PAIRS, i=2)
+                if b == 0:
+                    nc.vector.tensor_copy(out=chunk, in_=as_turned[:, e])
+                else:
+                    nc.scalar.copy(out=chunk, in_=as_turned[:, e])
 
         qT_ps, qT, s_ps, neg_max, row_sum, e_sb, eT_ps = {}, {}, {}, {}, {}, {}, {}
         grouped, e_codes, e_scales, inv_sum, acc, sum_sq, scaled, inv_rms = {}, {}, {}, {}, {}, {}, {}, {}
@@ -323,7 +327,7 @@ def tile_hopfieldmemorylayer_pb_t_e_kernel(
             for c in range(D_CHUNKS):
                 if live(i):
                     score(i, h, c)
-                if j == 0 and c < PAIRS:
+                if j == 0 and c < WORD_BLOCKS:
                     turn_keys(1, c)
                 if c == GAPS - 1 and h == 0 and live(i + 1):
                     for piece in range(HEADS * WORD_BLOCKS):
@@ -363,6 +367,6 @@ def tile_hopfieldmemorylayer_pb_t_e_kernel(
                 store_finished(ON_TENSOR, h)
 
             if j == -1:
-                for u in range(PAIRS):
-                    turn_keys(0, u)
+                for b in range(WORD_BLOCKS):
+                    turn_keys(0, b)
                     keep_warm(1)

from contextlib import ExitStack

import concourse.masks as masks
import concourse.mybir as mybir

F32 = mybir.dt.float32
BF16 = mybir.dt.bfloat16
I32 = mybir.dt.int32
U32 = mybir.dt.uint32
U8 = mybir.dt.uint8
FP8X4 = mybir.dt.float8_e4m3fn_x4
ALU = mybir.AluOpType
ACT = mybir.ActivationFunctionType
AXIS = mybir.AxisListType

P = 128
HEADS = 2
D = 512
SLOTS = 512
E = HEADS * D
ROWS = 2 * 2048
EPS = 1e-6
D_CHUNKS = D // P
PACK = 4
PAIRS = PACK // 2
BLOCK_TILES = 4
N_BLOCKS = ROWS // (P * BLOCK_TILES)
N_TILES = ROWS // P
GAPS = D_CHUNKS - 1
ON_TENSOR = N_TILES - 6
WARM_UP = 4
EARLY_FINISH = 4
LATE_FINISH = 5
WORD_BLOCKS = D // (2 * P)

FLOPS = 2 * 2 * ROWS * HEADS * D * SLOTS


def tile_hopfieldmemorylayer_pb_t_e_kernel(
    tc, q_scaled, k, v_words, v_scales, norm_retrieved_w, query_input, out
):
    nc = tc.nc

    by_block = "(n p t) f -> n p t f"
    q_blocks = q_scaled.rearrange("b s h d -> (b s) (h d)").rearrange(by_block, p=P, t=BLOCK_TILES)
    x_blocks = query_input.rearrange("b s f -> (b s) f").rearrange(by_block, p=P, t=BLOCK_TILES)
    out_blocks = out.rearrange("b s f -> (b s) f").rearrange(by_block, p=P, t=BLOCK_TILES)

    with ExitStack() as ctx:
        keep = ctx.enter_context(tc.tile_pool(name="keep", bufs=1))
        work = ctx.enter_context(tc.tile_pool(name="work", bufs=4))
        results = ctx.enter_context(tc.tile_pool(name="results", bufs=6))
        stats = ctx.enter_context(tc.tile_pool(name="stats", bufs=8))
        psum_turn = ctx.enter_context(tc.psum_pool(name="psum_turn", bufs=1))
        psum_scores = ctx.enter_context(tc.psum_pool(name="psum_scores", bufs=3))
        psum_acc = ctx.enter_context(tc.psum_pool(name="psum_acc", bufs=3))
        ctx.enter_context(tc.manual_schedule())

        zeros = keep.tile([P, SLOTS], BF16)
        nc.vector.memset(zeros[:], 0.0)

        def keep_warm(times):
            for turn in range(times):
                idle_ps = psum_acc.tile([P, SLOTS], F32, tag="acc")
                nc.tensor.matmul(idle_ps[:], lhsT=zeros[:, 0:P], rhs=zeros[:], start=True, stop=True)

        keep_warm(WARM_UP)
        v_planes = keep.tile([P, HEADS, D], U8, align_bytes=64)
        nc.vector.memset(v_planes[:].bitcast(I32), 0)
        minus_half = keep.tile([P, 1], F32)
        nc.vector.memset(minus_half[:], -0.5)
        minus_one = keep.tile([P, HEADS], F32)
        nc.vector.memset(minus_one[:], -1.0)
        ident_f32 = keep.tile([P, P], F32)
        masks.make_identity(nc, ident_f32[:])
        ident_bf = keep.tile([P, P], BF16)
        nc.gpsimd.tensor_copy(out=ident_bf[:], in_=ident_f32[:])
        table_warmer = keep.tile([P, 1], F32)
        nc.scalar.activation(out=table_warmer[:], in_=minus_half[:], func=ACT.Exp)

        q_sb = []
        x_sb = []
        for n in range(N_BLOCKS):
            q_sb.append(keep.tile([P, BLOCK_TILES, E], BF16, name="q_sb%d" % n))
            x_sb.append(keep.tile([P, BLOCK_TILES, E], BF16, name="x_sb%d" % n))
        k_sb = keep.tile([P, HEADS, PACK, D], BF16)
        k_by_slot_group = k.rearrange("h (p a) d -> h p a d", a=PACK)
        nc.sync.dma_start(out=q_sb[0][:, 0:1], in_=q_blocks[0][:, 0:1])
        nc.sync.dma_start(out=k_sb[:, 0], in_=k_by_slot_group[0])
        nc.sync.dma_start(out=k_sb[:, 1], in_=k_by_slot_group[1])
        nc.sync.dma_start(out=q_sb[0][:, 1:2], in_=q_blocks[0][:, 1:2])
        nc.sync.dma_start(out=q_sb[0][:, 2:], in_=q_blocks[0][:, 2:])
        v_codes = keep.tile([P, HEADS, D], U32, align_bytes=64)
        nc.sync.dma_start(
            out=v_codes[:].bitcast(I32),
            in_=v_words.rearrange("g p n t -> p g (n t)").bitcast(I32),
        )
        for quadrant in range(4):
            nc.sync.dma_start(
                out=v_planes[32 * quadrant : 32 * quadrant + 4].bitcast(I32),
                in_=v_scales[:, 4 * quadrant : 4 * quadrant + 4, :]
                .rearrange("g r n -> r g n")
                .bitcast(I32),
            )
        gain_bf = keep.tile([P, E], BF16)
        nc.sync.dma_start(out=gain_bf[:], in_=norm_retrieved_w.partition_broadcast(P))
        nc.sync.dma_start(out=q_sb[1][:], in_=q_blocks[1])
        nc.sync.dma_start(out=x_sb[0][:], in_=x_blocks[0])
        gain32 = keep.tile([P, HEADS, D], F32)
        nc.gpsimd.tensor_scalar(
            out=gain32[:].rearrange("p h d -> p (h d)"),
            in0=gain_bf[:],
            scalar1=float(E) ** 0.5,
            scalar2=0.0,
            op0=ALU.mult,
            op1=ALU.add,
        )

        kT = keep.tile([P, HEADS, D_CHUNKS, SLOTS], BF16)

        def turn_keys(h, b):
            if h == 0:
                kT_ps = psum_scores.tile([P, PACK, P], F32, tag="s_ps")
            else:
                kT_ps = psum_acc.tile([P, PACK, P], F32, tag="acc")
            for a in range(PACK):
                words = k_sb[:, h, a, :].bitcast(F32)
                nc.tensor.transpose(kT_ps[:, a, :], words[:, b * P : (b + 1) * P], ident_f32[:])
            in_order = "d (u p i) -> d u p i"
            as_turned = (
                kT_ps[:]
                .rearrange("d a p -> d (a p)")
                .bitcast(BF16)
                .rearrange("d (u i p e) -> d e u p i", u=PAIRS, i=2, e=2)
            )
            for e in range(2):
                chunk = kT[:, h, 2 * b + e, :].rearrange(in_order, u=PAIRS, i=2)
                if b == 0:
                    nc.vector.tensor_copy(out=chunk, in_=as_turned[:, e])
                else:
                    nc.scalar.copy(out=chunk, in_=as_turned[:, e])

        qT_ps, qT, s_ps, neg_max, row_sum, e_sb, eT_ps = {}, {}, {}, {}, {}, {}, {}
        grouped, e_codes, e_scales, inv_sum, acc, sum_sq, scaled, inv_rms = {}, {}, {}, {}, {}, {}, {}, {}

        def live(i):
            return 0 <= i < N_TILES

        def finish_lag(i):
            return EARLY_FINISH if i < N_TILES // 2 else LATE_FINISH

        def at(j, lag):
            return (j - lag) // HEADS, (j - lag) % HEADS

        def turn_q(i, j):
            if j == 0:
                qT_ps[i] = psum_turn.tile([P, HEADS * WORD_BLOCKS, P], F32, name="qT_ps")
            words = q_sb[i // BLOCK_TILES][:, i % BLOCK_TILES, :].bitcast(F32)
            nc.tensor.transpose(qT_ps[i][:, j, :], words[:, j * P : (j + 1) * P], ident_f32[:])

        def keep_qT(i):
            qT[i] = work.tile([P, HEADS * WORD_BLOCKS, P, 2], BF16, name="qT")
            nc.scalar.copy(
                out=qT[i][:].rearrange("p j r e -> p (j r e)").bitcast(F32),
                in_=qT_ps[i][:].rearrange("p j r -> p (j r)"),
            )

        def score(i, h, c):
            if c == 0:
                s_ps[i, h] = psum_scores.tile([P, SLOTS], F32, name="s_ps")
            nc.tensor.matmul(
                s_ps[i, h][:],
                lhsT=qT[i][:, WORD_BLOCKS * h + c // 2, :, c % 2],
                rhs=kT[:, h, c, :],
                start=(c == 0),
                stop=(c == D_CHUNKS - 1),
            )

        def row_max(i, h):
            if h == 0:
                neg_max[i] = stats.tile([P, HEADS], F32, name="neg_max")
            nc.vector.tensor_reduce(
                out=neg_max[i][:, h : h + 1], in_=s_ps[i, h][:], axis=AXIS.X, op=ALU.max, negate=True
            )

        def exponentials(i, h):
            if h == 0:
                row_sum[i] = stats.tile([P, HEADS], F32, name="row_sum")
                e_sb[i] = work.tile([P, HEADS, SLOTS], BF16, name="e_sb")
            nc.scalar.activation(
                out=e_sb[i][:, h, :],
                in_=s_ps[i, h][:],
                func=ACT.Exp,
                bias=neg_max[i][:, h : h + 1],
                scale=1.0,
                accum_out=row_sum[i][:, h : h + 1],
            )

        def turn_e(i, h, u):
            if h == 0 and u == 0:
                eT_ps[i] = psum_turn.tile([P, HEADS, PAIRS, P], F32, name="eT_ps")
            words = e_sb[i][:, h, :].bitcast(F32)
            nc.tensor.transpose(eT_ps[i][:, h, u, :], words[:, u * P : (u + 1) * P], ident_f32[:])

        def group_e(i):
            grouped[i] = work.tile([P, HEADS, P, PACK], BF16, name="grouped", align_bytes=64)
            nc.scalar.copy(
                out=grouped[i][:]
                .rearrange("p h r t -> p (h r t)")
                .bitcast(F32)
                .rearrange("p (h r u) -> p h r u", h=HEADS, u=PAIRS),
                in_=eT_ps[i][:].rearrange("p h u r -> p h r u"),
            )

        def quantise_e(i):
            e_codes[i] = work.tile([P, HEADS * P], U32, name="e_codes", align_bytes=64)
            e_scales[i] = work.tile([P, HEADS * P], U8, name="e_scales", align_bytes=64)
            nc.vector.quantize_mx(
                out=e_codes[i][:].bitcast(FP8X4),
                scales=e_scales[i][:],
                in_=grouped[i][:].rearrange("p h r t -> p (h r t)"),
            )

        def invert_row_sum(i):
            inv_sum[i] = stats.tile([P, HEADS], F32, name="inv_sum")
            nc.gpsimd.tensor_tensor(out=inv_sum[i][:], in0=row_sum[i][:], in1=minus_one[:], op=ALU.pow)

        def retrieve(i, h):
            acc[i, h] = psum_acc.tile([P, D], F32, name="acc")
            rows = slice(h * P, (h + 1) * P)
            nc.tensor.matmul_mx(
                out=acc[i, h][:],
                lhsT=e_codes[i][:, rows].bitcast(FP8X4),
                lhsT_scale=e_scales[i][:, rows],
                rhs=v_codes[:, h, :].bitcast(FP8X4),
                rhs_scale=v_planes[:, h, :],
                start=True,
                stop=True,
            )

        def apply_gain(i, h):
            if h == 0:
                scaled[i] = results.tile([P, HEADS, D], F32, name="scaled")
            nc.vector.scalar_tensor_tensor(
                out=scaled[i][:, h, :],
                in0=acc[i, h][:],
                scalar=inv_sum[i][:, h : h + 1],
                in1=gain32[:, h, :],
                op0=ALU.mult,
                op1=ALU.mult,
            )

        def sum_squares(i, h):
            if h == 0:
                sum_sq[i] = stats.tile([P, HEADS], F32, name="sum_sq")
            squares = work.tile([P, D], BF16, name="squares")
            nc.scalar.activation(
                out=squares[:],
                in_=acc[i, h][:],
                func=ACT.Square,
                scale=inv_sum[i][:, h : h + 1],
                accum_out=sum_sq[i][:, h : h + 1],
            )
            if h == HEADS - 1:
                total = stats.tile([P, 1], F32, name="total")
                nc.gpsimd.tensor_scalar(
                    out=total[:],
                    in0=sum_sq[i][:, 0:1],
                    scalar1=sum_sq[i][:, 1:2],
                    scalar2=E * EPS,
                    op0=ALU.add,
                    op1=ALU.add,
                )
                inv_rms[i] = stats.tile([P, 1], F32, name="inv_rms")
                nc.gpsimd.tensor_tensor(out=inv_rms[i][:], in0=total[:], in1=minus_half[:], op=ALU.pow)

        def finish(i):
            n, t = i // BLOCK_TILES, i % BLOCK_TILES
            row = scaled[i][:].rearrange("p h d -> p (h d)")
            width = E // 4 if i == N_TILES - 1 else E
            for start in range(0, E, width):
                columns = slice(start, start + width)
                nc.vector.scalar_tensor_tensor(
                    out=row[:, columns],
                    in0=row[:, columns],
                    scalar=inv_rms[i][:, 0:1],
                    in1=x_sb[n][:, t, columns],
                    op0=ALU.mult,
                    op1=ALU.add,
                )
                nc.sync.dma_start(out=out_blocks[n][:, t, columns], in_=row[:, columns])

        spread, finished = {}, {}

        def spread_factor(i):
            spread[i] = work.tile([P, P], F32, name="spread")
            nc.scalar.activation(out=spread[i][:], in_=ident_f32[:], func=ACT.Copy, scale=inv_rms[i][:, 0:1])

        def finish_on_tensor(i, h):
            n, t = i // BLOCK_TILES, i % BLOCK_TILES
            residual = x_sb[n][:, t, h * D : (h + 1) * D]
            finished[i, h] = psum_scores.tile([P, D], F32, name="s_ps")
            nc.tensor.matmul(finished[i, h][:], lhsT=ident_bf[:], rhs=residual, start=True, stop=False)
            nc.tensor.matmul(finished[i, h][:], lhsT=spread[i][:], rhs=scaled[i][:, h, :], start=False, stop=True)

        def store_finished(i, h):
            n, t = i // BLOCK_TILES, i % BLOCK_TILES
            nc.scalar.copy(out=scaled[i][:, h, :], in_=finished[i, h][:])
            nc.sync.dma_start(out=out_blocks[n][:, t, h * D : (h + 1) * D], in_=scaled[i][:, h, :])

        for j in range(-2, HEADS * (N_TILES + LATE_FINISH) + 2):
            i, h = at(j, 0)

            if live(i) and j % (HEADS * BLOCK_TILES) == 0:
                n = i // BLOCK_TILES
                if n + 2 < N_BLOCKS:
                    nc.sync.dma_start(out=q_sb[n + 2][:], in_=q_blocks[n + 2])
                if n + 1 < N_BLOCKS:
                    nc.sync.dma_start(out=x_sb[n + 1][:], in_=x_blocks[n + 1])

            if live(at(j, 2)[0]):
                exponentials(*at(j, 2))
            if h == 1 and live(i - 3):
                for half in range(HEADS):
                    sum_squares(i - 3, half)

            for c in range(D_CHUNKS):
                if live(i):
                    score(i, h, c)
                if j == 0 and c < WORD_BLOCKS:
                    turn_keys(1, c)
                if c == GAPS - 1 and h == 0 and live(i + 1):
                    for piece in range(HEADS * WORD_BLOCKS):
                        turn_q(i + 1, piece)
                if c == GAPS - 1 and h == 1 and live(i - 1):
                    for piece in range(HEADS * PAIRS):
                        turn_e(i - 1, piece // PAIRS, piece % PAIRS)
            if h == 1 and live(i - 2):
                for half in range(HEADS):
                    retrieve(i - 2, half)

            if j == HEADS * N_TILES:
                spread_factor(ON_TENSOR)
            if j in (HEADS * N_TILES, HEADS * N_TILES + 1):
                finish_on_tensor(ON_TENSOR, h)

            if live(at(j, 1)[0]):
                row_max(*at(j, 1))
            if h == 0 and live(i - 3):
                for half in range(HEADS):
                    apply_gain(i - 3, half)
            for lag in (EARLY_FINISH, LATE_FINISH):
                if h == 1 and live(i - lag) and finish_lag(i - lag) == lag and i - lag != ON_TENSOR:
                    finish(i - lag)
            if h == 0 and live(i - 2):
                quantise_e(i - 2)

            if h == 0 and live(i - 2):
                invert_row_sum(i - 2)

            if h == 1 and live(i + 1):
                keep_qT(i + 1)
            if h == 1 and live(i - 1):
                group_e(i - 1)

            if j - HEADS in (HEADS * N_TILES, HEADS * N_TILES + 1):
                store_finished(ON_TENSOR, h)

            if j == -1:
                for b in range(WORD_BLOCKS):
                    turn_keys(0, b)
                    keep_warm(1)
